import numpy as np
import ml_dtypes


BF16 = ml_dtypes.bfloat16


def bf(x):
    return np.asarray(x, np.float32).astype(BF16)


def f64(x):
    return np.asarray(x).astype(np.float64)


E2M1 = np.array([0.0, 0.5, 1.0, 1.5, 2.0, 3.0, 4.0, 6.0, -0.0, -0.5, -1.0, -1.5, -2.0, -3.0, -4.0, -6.0])


def pack_weight(w, fmt):
    k, n = w.shape
    w = f64(bf(w)).reshape(k // 32, 32, n)
    amax = np.abs(w).max(1)
    if fmt == "e4m3":
        byte = np.frexp(amax)[1] - 1 + 127 - 7
    else:
        mant, ex = np.frexp(amax / 6.0)
        byte = np.where(mant > 0.5, ex, ex - 1) + 127
    byte = np.clip(np.where(amax > 0, byte, 1), 1, 254)
    scaled = (w * np.exp2(127.0 - byte)[:, None, :]).reshape(k, n).astype(np.float32)
    by_word = np.ascontiguousarray(scaled.reshape(k // 512, 128, 4, n).transpose(0, 1, 3, 2))
    if fmt == "e4m3":
        words = by_word.astype(ml_dtypes.float8_e4m3fn).view(np.uint8)
    else:
        c = by_word.astype(ml_dtypes.float4_e2m1fn).view(np.uint8) & 0xF
        words = c[..., 0::2] | (c[..., 1::2] << 4)
    return np.ascontiguousarray(words), np.ascontiguousarray(byte.astype(np.uint8).reshape(k // 512, 16, n))


def unpack_weight(words, scales, fmt):
    g, p, n, _ = words.shape
    if fmt == "e4m3":
        vals = np.ascontiguousarray(words).view(ml_dtypes.float8_e4m3fn).astype(np.float64)
    else:
        nib = np.empty((g, p, n, 4), np.uint8)
        nib[..., 0::2] = words & 0xF
        nib[..., 1::2] = words >> 4
        vals = E2M1[nib]
    vals = vals * np.repeat(np.exp2(scales.astype(np.float64) - 127.0), 8, axis=1)[..., None]
    return vals.transpose(0, 1, 3, 2).reshape(g * 512, n)

def pack4(w):
    words, scales = pack_weight(w, "e2m1")
    return words.reshape(words.shape[0], 128, -1), scales


def unpack4(words, scales):
    return unpack_weight(words.reshape(words.shape[0], 128, -1, 2), scales, "e2m1")


def kspread(k):
    return np.exp2(np.repeat(np.random.randint(-6, 7, k // 32), 32).astype(np.float64))


B, S, HID, H, KV, D, ROT, D_PAD = 8, 256, 4096, 2, 2, 128, 64, 128
T = B * S
HALF = ROT // 2
NQ = H * D
NK = KV * D


def partial_rope(x, cos, sin):
    x1 = x[:, :, :HALF]
    x2 = x[:, :, HALF:ROT]
    xp = x[:, :, ROT:]
    c = cos[:, None, :]
    s = sin[:, None, :]
    return np.concatenate([x1 * c - x2 * s, x2 * c + x1 * s, xp], axis=-1)


def setup_inputs():
    s = kspread(HID)
    hidden_states = np.random.standard_normal((T, HID)) * s
    hidden_states_words, hidden_states_scales = pack4(np.ascontiguousarray(hidden_states.T))
    cos = bf(np.random.uniform(size=(T, HALF)))
    sin = bf(np.random.uniform(size=(T, HALF)))
    w_qk = np.random.standard_normal((NQ + NK, HID)) / np.sqrt(HID) / s[None, :]
    words, scales = pack4(np.ascontiguousarray(w_qk.T))
    b_qk = bf(np.random.standard_normal(NQ + NK) * 0.3)
    return {"hidden_states_words": hidden_states_words,
            "hidden_states_scales": hidden_states_scales,
            "cos": cos,
            "sin": sin,
            "w_qk_words": words,
            "w_qk_scales": scales,
            "b_qk": b_qk}


def reference(hidden_states_words, hidden_states_scales, cos, sin, w_qk_words, w_qk_scales, b_qk):
    qk = (unpack4(hidden_states_words, hidden_states_scales).T @ unpack4(w_qk_words, w_qk_scales)) + f64(b_qk)
    q = qk[:, :NQ].reshape(T, H, D)
    k = qk[:, NQ:].reshape(T, KV, D)
    c = f64(cos)
    s = f64(sin)
    return partial_rope(q, c, s), partial_rope(k, c, s)

@@ -1,0 +1,255 @@
+from contextlib import ExitStack
+
+import concourse.mybir as mybir
+
+FLOPS = 2 * 2048 * 4096 * 512
+
+F32 = mybir.dt.float32
+BF16 = mybir.dt.bfloat16
+U8 = mybir.dt.uint8
+I32 = mybir.dt.int32
+FP4X4 = mybir.dt.float4_e2m1fn_x4
+ADD = mybir.AluOpType.add
+MULT = mybir.AluOpType.mult
+
+P = 128
+PASSES = 8
+CH = 512
+HEADS = 4
+D = 128
+ROT = 64
+HALF = 32
+TILES = 16
+N_WARM = 6
+
+CHUNKS = [(0, 6), (6, 9), (9, 12), (12, 16)]
+SWEEP_TILES = 6
+SWEEP_PASSES = 5
+FIRST_CODE_RUNS = [(0, 1), (1, 2), (2, 4), (4, 6), (6, 8)]
+FIRST_SCALE_RUNS = [(0, 4), (4, 8)]
+LEAD_TILES = 2
+LAST_PIECES = [(0, 2), (2, 2)]
+
+
+def load_codes(nc, dst, words, g0, g1, b0, b1):
+    nc.sync.dma_start(
+        out=dst[:, :, :].bitcast(I32),
+        in_=words[g0:g1, :, b0:b1].rearrange("g p c -> p g c").bitcast(I32),
+    )
+
+
+def load_scales(nc, dst, scales, g0, g1, c0, c1):
+    for q in range(4):
+        nc.sync.dma_start(
+            out=dst[32 * q : 32 * q + 4, :, :].bitcast(I32),
+            in_=scales[g0:g1, 4 * q : 4 * q + 4, c0:c1].rearrange("g r n -> r g n").bitcast(I32),
+        )
+
+
+def tile_flashphiattention_pa_t_kernel(
+    tc, hidden_states_words, hidden_states_scales, cos, sin, w_qk_words, w_qk_scales, b_qk, out_0, out_1
+):
+    nc = tc.nc
+    with ExitStack() as ctx:
+        ctx.enter_context(tc.manual_schedule())
+        keep = ctx.enter_context(tc.tile_pool(name="keep", bufs=1))
+        work = ctx.enter_context(tc.tile_pool(name="work", bufs=3))
+        outs = ctx.enter_context(tc.tile_pool(name="outs", bufs=8))
+        psum = ctx.enter_context(tc.psum_pool(name="psum", bufs=7))
+        psum_aux = ctx.enter_context(tc.psum_pool(name="psum_aux", bufs=1))
+
+        chunk_of = {}
+        for c, (lo, hi) in enumerate(CHUNKS):
+            for i in range(lo, hi):
+                chunk_of[i] = c
+        tok0 = (CHUNKS[0][1] - CHUNKS[0][0]) * P
+
+        w_code = {}
+        w_plane = {}
+        h_code = {}
+        h_plane = {}
+        planes_in_order = []
+        for g0, g1 in FIRST_SCALE_RUNS:
+            wp = keep.tile([P, g1 - g0, CH], U8, name="wp%d" % g0, tag="wp%d" % g0, align_bytes=256)
+            hp = keep.tile([P, g1 - g0, tok0], U8, name="hp0_%d" % g0, tag="hp0_%d" % g0, align_bytes=256)
+            planes_in_order.append(wp)
+            planes_in_order.append(hp)
+            for g in range(g0, g1):
+                w_plane[g] = (wp, g - g0)
+                h_plane[(0, g)] = (hp, g - g0)
+        for c in range(1, len(CHUNKS)):
+            ntok = (CHUNKS[c][1] - CHUNKS[c][0]) * P
+            hp = keep.tile([P, PASSES, ntok], U8, name="hp%d" % c, tag="hp%d" % c, align_bytes=256)
+            planes_in_order.append(hp)
+            for g in range(PASSES):
+                h_plane[(c, g)] = (hp, g)
+        for g0, g1 in FIRST_CODE_RUNS:
+            wc = keep.tile([P, g1 - g0, 2 * CH], U8, name="wc%d" % g0, tag="wc%d" % g0, align_bytes=256)
+            hc = keep.tile([P, g1 - g0, 2 * tok0], U8, name="hc0_%d" % g0, tag="hc0_%d" % g0, align_bytes=256)
+            for g in range(g0, g1):
+                w_code[g] = (wc, g - g0)
+                h_code[(0, g)] = (hc, g - g0)
+        lead = keep.tile([P, 1, 2 * LEAD_TILES * P], U8, name="lead", tag="lead", align_bytes=256)
+        for c in range(1, len(CHUNKS)):
+            ntok = (CHUNKS[c][1] - CHUNKS[c][0]) * P
+            hc = keep.tile([P, PASSES, 2 * ntok], U8, name="hc%d" % c, tag="hc%d" % c, align_bytes=256)
+            for g in range(PASSES):
+                h_code[(c, g)] = (hc, g)
+
+        ones = keep.tile([P, CH], BF16, name="ones", tag="ones")
+        brow = keep.tile([P, CH], BF16, name="brow", tag="brow")
+        bias = keep.tile([P, CH], F32, name="bias", tag="bias")
+        cos_a = keep.tile([P, SWEEP_TILES, HALF], BF16, name="cos_a", tag="cos_a")
+        cos_b = keep.tile([P, TILES - SWEEP_TILES, HALF], BF16, name="cos_b", tag="cos_b")
+        ss_a = keep.tile([P, SWEEP_TILES, 2, HALF], BF16, name="ss_a", tag="ss_a")
+        ss_b = keep.tile([P, TILES - SWEEP_TILES, 2, HALF], BF16, name="ss_b", tag="ss_b")
+
+        nc.vector.memset(ones[:, :], 1.0)
+        nc.vector.memset(planes_in_order[0][:, :, :].bitcast(I32), 0)
+        nc.vector.memset(planes_in_order[1][:, :, :].bitcast(I32), 0)
+        nc.vector.memset(brow[:, :], 0.0)
+        for pl in planes_in_order[2:]:
+            nc.vector.memset(pl[:, :, :].bitcast(I32), 0)
+
+        cos_v = cos.rearrange("(i p) j -> p i j", p=P)
+        sin_v = sin.rearrange("(i p) j -> p i j", p=P)
+
+        def first_codes(k):
+            g0, g1 = FIRST_CODE_RUNS[k]
+            load_codes(nc, w_code[g0][0], w_qk_words, g0, g1, 0, 2 * CH)
+            load_codes(nc, h_code[(0, g0)][0], hidden_states_words, g0, g1, 0, 2 * tok0)
+
+        def first_scales(k):
+            g0, g1 = FIRST_SCALE_RUNS[k]
+            load_scales(nc, w_plane[g0][0], w_qk_scales, g0, g1, 0, CH)
+            load_scales(nc, h_plane[(0, g0)][0], hidden_states_scales, g0, g1, 0, tok0)
+
+        load_codes(nc, w_code[0][0], w_qk_words, 0, 1, 0, 2 * CH)
+        load_codes(nc, lead, hidden_states_words, 0, 1, 0, 2 * LEAD_TILES * P)
+        first_scales(0)
+        nc.sync.dma_start(
+            out=h_code[(0, 0)][0][:, :, 2 * LEAD_TILES * P : 2 * tok0].bitcast(I32),
+            in_=hidden_states_words[0:1, :, 2 * LEAD_TILES * P : 2 * tok0].rearrange("g p c -> p g c").bitcast(I32),
+        )
+        first_codes(1)
+        first_codes(2)
+        nc.sync.dma_start(out=brow[0:1, :], in_=b_qk.unsqueeze(0))
+        first_scales(1)
+        first_codes(3)
+        first_codes(4)
+        nc.sync.dma_start(out=cos_a[:, :, :], in_=cos_v[:, 0:SWEEP_TILES, :])
+        nc.sync.dma_start(out=ss_a[:, :, 1, :], in_=sin_v[:, 0:SWEEP_TILES, :])
+        for c in range(1, len(CHUNKS)):
+            t0 = CHUNKS[c][0] * P
+            t1 = CHUNKS[c][1] * P
+            load_scales(nc, h_plane[(c, 0)][0], hidden_states_scales, 0, PASSES, t0, t1)
+            load_codes(nc, h_code[(c, 0)][0], hidden_states_words, 0, PASSES, 2 * t0, 2 * t1)
+            if c == 1:
+                nc.sync.dma_start(out=cos_b[:, :, :], in_=cos_v[:, SWEEP_TILES:TILES, :])
+                nc.sync.dma_start(out=ss_b[:, :, 1, :], in_=sin_v[:, SWEEP_TILES:TILES, :])
+
+        def mm(acc, i, g, n0, n1):
+            c = chunk_of[i]
+            t = i - CHUNKS[c][0]
+            hc, hg = (lead, 0) if (g == 0 and i < LEAD_TILES) else h_code[(c, g)]
+            hp, hpg = h_plane[(c, g)]
+            wc, wg = w_code[g]
+            wp, wpg = w_plane[g]
+            nc.tensor.matmul_mx(
+                out=acc,
+                lhsT=hc[:, hg, 2 * P * t : 2 * P * (t + 1)].bitcast(FP4X4),
+                lhsT_scale=hp[:, hpg, P * t : P * (t + 1)],
+                rhs=wc[:, wg, 2 * n0 : 2 * n1].bitcast(FP4X4),
+                rhs_scale=wp[:, wpg, n0:n1],
+                start=(g == 0),
+                stop=(g == PASSES - 1),
+            )
+
+        def add_bias(i, acc, h0, nh):
+            o = outs.tile([P, nh, D], F32, name="o", tag="o")
+            nc.vector.tensor_tensor(
+                out=o[:, :, :],
+                in0=acc.rearrange("p (h d) -> p h d", d=D),
+                in1=bias[:, h0 * D : (h0 + nh) * D].rearrange("p (h d) -> p h d", d=D),
+                op=ADD,
+            )
+            return (i, o, h0, nh)
+
+        def rotate_products(state):
+            i, o, h0, nh = state
+            ct, st, ii = (cos_a, ss_a, i) if i < SWEEP_TILES else (cos_b, ss_b, i - SWEEP_TILES)
+            y = o[:, :, 0:ROT].rearrange("p h (a j) -> p h a j", a=2)
+            a = work.tile([P, nh, 2, HALF], F32, name="a", tag="a")
+            b = work.tile([P, nh, 2, HALF], F32, name="b", tag="b")
+            nc.vector.tensor_tensor(
+                out=a[:, :, :, :],
+                in0=y,
+                in1=ct[:, ii, :].unsqueeze(1).unsqueeze(1).to_broadcast([P, nh, 2, HALF]),
+                op=MULT,
+            )
+            nc.vector.tensor_tensor(
+                out=b[:, :, :, :],
+                in0=y[:, :, ::-1, :],
+                in1=st[:, ii, :, :].unsqueeze(1).to_broadcast([P, nh, 2, HALF]),
+                op=MULT,
+            )
+            return (i, o, h0, nh, a, b)
+
+        def finish(state, queue):
+            i, o, h0, nh, a, b = state
+            nc.vector.tensor_tensor(
+                out=o[:, :, 0:ROT],
+                in0=a[:, :, :, :].rearrange("p h a j -> p h (a j)"),
+                in1=b[:, :, :, :].rearrange("p h a j -> p h (a j)"),
+                op=ADD,
+            )
+            rows = slice(i * P, (i + 1) * P)
+            for dst, lo in ((out_0, 0), (out_1, 2)):
+                s0 = max(h0, lo)
+                s1 = min(h0 + nh, lo + 2)
+                if s0 < s1:
+                    queue.dma_start(out=dst[rows, s0 - lo : s1 - lo, :], in_=o[:, s0 - h0 : s1 - h0, :])
+
+        pending = []
+
+        def epilogue(i, acc, h0, nh, queue):
+            state = add_bias(i, acc, h0, nh)
+            if pending:
+                finish(pending[0][0], pending[0][1])
+                pending.clear()
+            if i == 0:
+                nc.vector.tensor_scalar_mul(out=ss_a[:, :, 0, :], in0=ss_a[:, :, 1, :], scalar1=-1.0)
+            if i == SWEEP_TILES:
+                nc.vector.tensor_scalar_mul(out=ss_b[:, :, 0, :], in0=ss_b[:, :, 1, :], scalar1=-1.0)
+            pending.append((rotate_products(state), queue))
+
+        aux = psum_aux.tile([P, CH], F32, name="aux", tag="aux")
+        for d in range(N_WARM):
+            nc.tensor.matmul(out=aux[:, :], lhsT=ones[:, 0:P], rhs=ones[:, :], start=True, stop=True)
+
+        first = []
+        for t in range(SWEEP_TILES):
+            acc = psum.tile([P, CH], F32, name="acc_f%d" % t, tag="acc")
+            first.append(acc)
+        for g in range(SWEEP_PASSES):
+            for t in range(SWEEP_TILES):
+                mm(first[t][:, :], t, g, 0, CH)
+            if g == 2:
+                nc.tensor.matmul(out=aux[:, :], lhsT=ones[:, 0:P], rhs=brow[:, :], start=True, stop=True)
+                nc.vector.tensor_copy(out=bias[:, :], in_=aux[:, :])
+        for t in range(SWEEP_TILES):
+            for g in range(SWEEP_PASSES, PASSES):
+                mm(first[t][:, :], t, g, 0, CH)
+            epilogue(t, first[t][:, :], 0, HEADS, nc.sync)
+        for i in range(SWEEP_TILES, TILES - 1):
+            acc = psum.tile([P, CH], F32, name="acc", tag="acc")
+            for g in range(PASSES):
+                mm(acc[:, :], i, g, 0, CH)
+            epilogue(i, acc[:, :], 0, HEADS, nc.sync)
+        i = TILES - 1
+        for k, (h0, nh) in enumerate(LAST_PIECES):
+            acc = psum.tile([P, nh * D], F32, name="acc_l", tag="acc")
+            for g in range(PASSES):
+                mm(acc[:, :], i, g, h0 * D, (h0 + nh) * D)
+            epilogue(i, acc[:, :], h0, nh, nc.sync)
+        finish(pending[0][0], pending[0][1])

@@ -28,7 +28,7 @@ SWEEP_PASSES = 5
 FIRST_CODE_RUNS = [(0, 1), (1, 2), (2, 4), (4, 6), (6, 8)]
 FIRST_SCALE_RUNS = [(0, 4), (4, 8)]
 LEAD_TILES = 2
-LAST_PIECES = [(0, 2), (2, 2)]
+SPLIT_TILES = 4
 
 
 def load_codes(nc, dst, words, g0, g1, b0, b1):
@@ -95,6 +95,9 @@ def tile_flashphiattention_pa_t_kernel(
             hc = keep.tile([P, PASSES, 2 * ntok], U8, name="hc%d" % c, tag="hc%d" % c, align_bytes=256)
             for g in range(PASSES):
                 h_code[(c, g)] = (hc, g)
+
+        wq_code = keep.tile([P, PASSES, 2 * CH], U8, name="wq_code", tag="wq_code", align_bytes=256)
+        wq_plane = keep.tile([P, PASSES, CH], U8, name="wq_plane", tag="wq_plane", align_bytes=256)
 
         ones = keep.tile([P, CH], BF16, name="ones", tag="ones")
         brow = keep.tile([P, CH], BF16, name="brow", tag="brow")
@@ -165,18 +168,57 @@ def tile_flashphiattention_pa_t_kernel(
                 stop=(g == PASSES - 1),
             )
 
-        def add_bias(i, acc, h0, nh):
-            o = outs.tile([P, nh, D], F32, name="o", tag="o")
+        def mm_q(acc, i, g, n0, n1):
+            c = chunk_of[i]
+            t = i - CHUNKS[c][0]
+            hc, hg = h_code[(c, g)]
+            hp, hpg = h_plane[(c, g)]
+            nc.tensor.matmul_mx(
+                out=acc,
+                lhsT=hc[:, hg, 2 * P * t : 2 * P * (t + 1)].bitcast(FP4X4),
+                lhsT_scale=hp[:, hpg, P * t : P * (t + 1)],
+                rhs=wq_code[:, g, 2 * n0 : 2 * n1].bitcast(FP4X4),
+                rhs_scale=wq_plane[:, g, n0:n1],
+                start=(g == 0),
+                stop=(g == PASSES - 1),
+            )
+
+        def permute_w():
+            for runs, table, dst, width in (
+                (FIRST_CODE_RUNS, w_code, wq_code, 2 * CH),
+                (FIRST_SCALE_RUNS, w_plane, wq_plane, CH),
+            ):
+                for g0, g1 in runs:
+                    for a in range(2):
+                        nc.vector.tensor_copy(
+                            out=dst[:, g0:g1, a * (width // 2) : (a + 1) * (width // 2)]
+                            .bitcast(I32)
+                            .rearrange("p g (h c) -> p g h c", h=HEADS),
+                            in_=table[g0][0][:, :, :]
+                            .bitcast(I32)
+                            .rearrange("p g (h a c) -> p g h a c", h=HEADS, a=2)[:, :, :, a, :],
+                        )
+
+        def add_bias(i, acc, c0, c1, h0=0, nh=HEADS):
+            o = outs.tile([P, nh, c1 - c0], F32, name="o", tag="o")
             nc.vector.tensor_tensor(
                 out=o[:, :, :],
-                in0=acc.rearrange("p (h d) -> p h d", d=D),
-                in1=bias[:, h0 * D : (h0 + nh) * D].rearrange("p (h d) -> p h d", d=D),
+                in0=acc.rearrange("p (h d) -> p h d", h=nh),
+                in1=bias[:, :].rearrange("p (h d) -> p h d", h=HEADS)[:, h0 : h0 + nh, c0:c1],
                 op=ADD,
             )
-            return (i, o, h0, nh)
+            return (i, o, c0, c1)
+
+        def store(i, o, c0, c1, queue, h0=0, nh=HEADS):
+            rows = slice(i * P, (i + 1) * P)
+            if h0 < 2:
+                queue.dma_start(out=out_0[rows, :, c0:c1], in_=o[:, 0:2, :])
+            if h0 + nh > 2:
+                queue.dma_start(out=out_1[rows, :, c0:c1], in_=o[:, 2 - h0 : 4 - h0, :])
 
         def rotate_products(state):
-            i, o, h0, nh = state
+            i, o, c0, c1 = state
+            nh = HEADS
             ct, st, ii = (cos_a, ss_a, i) if i < SWEEP_TILES else (cos_b, ss_b, i - SWEEP_TILES)
             y = o[:, :, 0:ROT].rearrange("p h (a j) -> p h a j", a=2)
             a = work.tile([P, nh, 2, HALF], F32, name="a", tag="a")
@@ -193,27 +235,22 @@ def tile_flashphiattention_pa_t_kernel(
                 in1=st[:, ii, :, :].unsqueeze(1).to_broadcast([P, nh, 2, HALF]),
                 op=MULT,
             )
-            return (i, o, h0, nh, a, b)
+            return (i, o, c0, c1, a, b)
 
         def finish(state, queue):
-            i, o, h0, nh, a, b = state
+            i, o, c0, c1, a, b = state
             nc.vector.tensor_tensor(
                 out=o[:, :, 0:ROT],
                 in0=a[:, :, :, :].rearrange("p h a j -> p h (a j)"),
                 in1=b[:, :, :, :].rearrange("p h a j -> p h (a j)"),
                 op=ADD,
             )
-            rows = slice(i * P, (i + 1) * P)
-            for dst, lo in ((out_0, 0), (out_1, 2)):
-                s0 = max(h0, lo)
-                s1 = min(h0 + nh, lo + 2)
-                if s0 < s1:
-                    queue.dma_start(out=dst[rows, s0 - lo : s1 - lo, :], in_=o[:, s0 - h0 : s1 - h0, :])
+            store(i, o, c0, c1, queue)
 
         pending = []
 
-        def epilogue(i, acc, h0, nh, queue):
-            state = add_bias(i, acc, h0, nh)
+        def epilogue(i, acc, c0, c1, queue):
+            state = add_bias(i, acc, c0, c1)
             if pending:
                 finish(pending[0][0], pending[0][1])
                 pending.clear()
@@ -240,16 +277,27 @@ def tile_flashphiattention_pa_t_kernel(
         for t in range(SWEEP_TILES):
             for g in range(SWEEP_PASSES, PASSES):
                 mm(first[t][:, :], t, g, 0, CH)
-            epilogue(t, first[t][:, :], 0, HEADS, nc.sync)
-        for i in range(SWEEP_TILES, TILES - 1):
+            if t == 0:
+                permute_w()
+            epilogue(t, first[t][:, :], 0, D, nc.sync)
+        for i in range(SWEEP_TILES, TILES - SPLIT_TILES):
             acc = psum.tile([P, CH], F32, name="acc", tag="acc")
             for g in range(PASSES):
                 mm(acc[:, :], i, g, 0, CH)
-            epilogue(i, acc[:, :], 0, HEADS, nc.sync)
-        i = TILES - 1
-        for k, (h0, nh) in enumerate(LAST_PIECES):
-            acc = psum.tile([P, nh * D], F32, name="acc_l", tag="acc")
+            epilogue(i, acc[:, :], 0, D, nc.sync)
+        for i in range(TILES - SPLIT_TILES, TILES):
+            acc = psum.tile([P, HEADS * ROT], F32, name="acc_r", tag="acc")
             for g in range(PASSES):
-                mm(acc[:, :], i, g, h0 * D, (h0 + nh) * D)
-            epilogue(i, acc[:, :], h0, nh, nc.sync)
-        finish(pending[0][0], pending[0][1])
+                mm_q(acc[:, :], i, g, 0, HEADS * ROT)
+            epilogue(i, acc[:, :], 0, ROT, nc.sync)
+        for i in range(TILES - SPLIT_TILES, TILES):
+            for h0, nh in ([(0, HEADS)] if i < TILES - 1 else [(0, 2), (2, 2)]):
+                acc = psum.tile([P, nh * (D - ROT)], F32, name="acc_x", tag="acc")
+                n0 = HEADS * ROT + h0 * (D - ROT)
+                for g in range(PASSES):
+                    mm_q(acc[:, :], i, g, n0, n0 + nh * (D - ROT))
+                state = add_bias(i, acc[:, :], ROT, D, h0, nh)
+                store(state[0], state[1], state[2], state[3], nc.sync, h0, nh)
+                if pending:
+                    finish(pending[0][0], pending[0][1])
+                    pending.clear()

@@ -39,10 +39,10 @@ def load_codes(nc, dst, words, g0, g1, b0, b1):
 
 
 def load_scales(nc, dst, scales, g0, g1, c0, c1):
-    for q in range(4):
+    for r in range(4):
         nc.sync.dma_start(
-            out=dst[32 * q : 32 * q + 4, :, :].bitcast(I32),
-            in_=scales[g0:g1, 4 * q : 4 * q + 4, c0:c1].rearrange("g r n -> r g n").bitcast(I32),
+            out=dst[r : P : 32, :, :].bitcast(I32),
+            in_=scales[g0:g1, r : 16 : 4, c0:c1].rearrange("g q n -> q g n").bitcast(I32),
         )
 
 

@@ -70,8 +70,8 @@ def tile_flashphiattention_pa_t_kernel(
         h_plane = {}
         planes_in_order = []
         for g0, g1 in FIRST_SCALE_RUNS:
-            wp = keep.tile([P, g1 - g0, CH], U8, name="wp%d" % g0, tag="wp%d" % g0, align_bytes=256)
-            hp = keep.tile([P, g1 - g0, tok0], U8, name="hp0_%d" % g0, tag="hp0_%d" % g0, align_bytes=256)
+            wp = keep.tile([P, g1 - g0, CH], U8, name="wp%d" % g0, tag="wp%d" % g0, align_bytes=1024)
+            hp = keep.tile([P, g1 - g0, tok0], U8, name="hp0_%d" % g0, tag="hp0_%d" % g0, align_bytes=1024)
             planes_in_order.append(wp)
             planes_in_order.append(hp)
             for g in range(g0, g1):
@@ -79,25 +79,25 @@ def tile_flashphiattention_pa_t_kernel(
                 h_plane[(0, g)] = (hp, g - g0)
         for c in range(1, len(CHUNKS)):
             ntok = (CHUNKS[c][1] - CHUNKS[c][0]) * P
-            hp = keep.tile([P, PASSES, ntok], U8, name="hp%d" % c, tag="hp%d" % c, align_bytes=256)
+            hp = keep.tile([P, PASSES, ntok], U8, name="hp%d" % c, tag="hp%d" % c, align_bytes=1024)
             planes_in_order.append(hp)
             for g in range(PASSES):
                 h_plane[(c, g)] = (hp, g)
         for g0, g1 in FIRST_CODE_RUNS:
-            wc = keep.tile([P, g1 - g0, 2 * CH], U8, name="wc%d" % g0, tag="wc%d" % g0, align_bytes=256)
-            hc = keep.tile([P, g1 - g0, 2 * tok0], U8, name="hc0_%d" % g0, tag="hc0_%d" % g0, align_bytes=256)
+            wc = keep.tile([P, g1 - g0, 2 * CH], U8, name="wc%d" % g0, tag="wc%d" % g0, align_bytes=1024)
+            hc = keep.tile([P, g1 - g0, 2 * tok0], U8, name="hc0_%d" % g0, tag="hc0_%d" % g0, align_bytes=1024)
             for g in range(g0, g1):
                 w_code[g] = (wc, g - g0)
                 h_code[(0, g)] = (hc, g - g0)
-        lead = keep.tile([P, 1, 2 * LEAD_TILES * P], U8, name="lead", tag="lead", align_bytes=256)
+        lead = keep.tile([P, 1, 2 * LEAD_TILES * P], U8, name="lead", tag="lead", align_bytes=1024)
         for c in range(1, len(CHUNKS)):
             ntok = (CHUNKS[c][1] - CHUNKS[c][0]) * P
-            hc = keep.tile([P, PASSES, 2 * ntok], U8, name="hc%d" % c, tag="hc%d" % c, align_bytes=256)
+            hc = keep.tile([P, PASSES, 2 * ntok], U8, name="hc%d" % c, tag="hc%d" % c, align_bytes=1024)
             for g in range(PASSES):
                 h_code[(c, g)] = (hc, g)
 
-        wq_code = keep.tile([P, PASSES, 2 * CH], U8, name="wq_code", tag="wq_code", align_bytes=256)
-        wq_plane = keep.tile([P, PASSES, CH], U8, name="wq_plane", tag="wq_plane", align_bytes=256)
+        wq_code = keep.tile([P, PASSES, 2 * CH], U8, name="wq_code", tag="wq_code", align_bytes=1024)
+        wq_plane = keep.tile([P, PASSES, CH], U8, name="wq_plane", tag="wq_plane", align_bytes=1024)
 
         ones = keep.tile([P, CH], BF16, name="ones", tag="ones")
         brow = keep.tile([P, CH], BF16, name="brow", tag="brow")

@@ -100,8 +100,10 @@ def tile_flashphiattention_pa_t_kernel(
         wq_plane = keep.tile([P, PASSES, CH], U8, name="wq_plane", tag="wq_plane", align_bytes=1024)
 
         ones = keep.tile([P, CH], BF16, name="ones", tag="ones")
-        brow = keep.tile([P, CH], BF16, name="brow", tag="brow")
-        bias = keep.tile([P, CH], F32, name="bias", tag="bias")
+        brow = keep.tile([P, CH], BF16, name="brow", tag="brow", align_bytes=64)
+        bcol = keep.tile([P, CH], BF16, name="bcol", tag="bcol", align_bytes=64)
+        bwide = keep.tile([P, CH], BF16, name="bwide", tag="bwide", align_bytes=64)
+        bias = keep.tile([P, CH], BF16, name="bias", tag="bias", align_bytes=64)
         cos_a = keep.tile([P, SWEEP_TILES, HALF], BF16, name="cos_a", tag="cos_a")
         cos_b = keep.tile([P, TILES - SWEEP_TILES, HALF], BF16, name="cos_b", tag="cos_b")
         ss_a = keep.tile([P, SWEEP_TILES, 2, HALF], BF16, name="ss_a", tag="ss_a")
@@ -136,7 +138,7 @@ def tile_flashphiattention_pa_t_kernel(
         )
         first_codes(1)
         first_codes(2)
-        nc.sync.dma_start(out=brow[0:1, :], in_=b_qk.unsqueeze(0))
+        nc.sync.dma_start(out=brow[0:P:32, :], in_=b_qk.partition_broadcast(4))
         first_scales(1)
         first_codes(3)
         first_codes(4)
@@ -272,8 +274,12 @@ def tile_flashphiattention_pa_t_kernel(
             for t in range(SWEEP_TILES):
                 mm(first[t][:, :], t, g, 0, CH)
             if g == 2:
-                nc.tensor.matmul(out=aux[:, :], lhsT=ones[:, 0:P], rhs=brow[:, :], start=True, stop=True)
-                nc.vector.tensor_copy(out=bias[:, :], in_=aux[:, :])
+                nc.vector.transpose(out=bcol[:, :], in_=brow[:, :])
+                nc.vector.tensor_copy(
+                    out=bwide[:, :].rearrange("p (c i) -> p c i", i=32),
+                    in_=bcol[:, :].rearrange("p (c i) -> p c i", i=32)[:, :, 0:1].to_broadcast([P, CH // 32, 32]),
+                )
+                nc.vector.transpose(out=bias[:, :], in_=bwide[:, :])
         for t in range(SWEEP_TILES):
             for g in range(SWEEP_PASSES, PASSES):
                 mm(first[t][:, :], t, g, 0, CH)

@@ -26,7 +26,7 @@ CHUNKS = [(0, 6), (6, 9), (9, 12), (12, 16)]
 SWEEP_TILES = 6
 SWEEP_PASSES = 5
 FIRST_CODE_RUNS = [(0, 1), (1, 2), (2, 4), (4, 6), (6, 8)]
-FIRST_SCALE_RUNS = [(0, 4), (4, 8)]
+FIRST_SCALE_RUNS = [(0, 3), (3, 8)]
 LEAD_TILES = 2
 SPLIT_TILES = 4
 

from contextlib import ExitStack

import concourse.mybir as mybir

FLOPS = 2 * 2048 * 4096 * 512

F32 = mybir.dt.float32
BF16 = mybir.dt.bfloat16
U8 = mybir.dt.uint8
I32 = mybir.dt.int32
FP4X4 = mybir.dt.float4_e2m1fn_x4
ADD = mybir.AluOpType.add
MULT = mybir.AluOpType.mult

P = 128
PASSES = 8
CH = 512
HEADS = 4
D = 128
ROT = 64
HALF = 32
TILES = 16
N_WARM = 6

CHUNKS = [(0, 6), (6, 9), (9, 12), (12, 16)]
SWEEP_TILES = 6
SWEEP_PASSES = 5
FIRST_CODE_RUNS = [(0, 1), (1, 2), (2, 4), (4, 6), (6, 8)]
FIRST_SCALE_RUNS = [(0, 3), (3, 8)]
LEAD_TILES = 2
SPLIT_TILES = 4


def load_codes(nc, dst, words, g0, g1, b0, b1):
    nc.sync.dma_start(
        out=dst[:, :, :].bitcast(I32),
        in_=words[g0:g1, :, b0:b1].rearrange("g p c -> p g c").bitcast(I32),
    )


def load_scales(nc, dst, scales, g0, g1, c0, c1):
    for r in range(4):
        nc.sync.dma_start(
            out=dst[r : P : 32, :, :].bitcast(I32),
            in_=scales[g0:g1, r : 16 : 4, c0:c1].rearrange("g q n -> q g n").bitcast(I32),
        )


def tile_flashphiattention_pa_t_kernel(
    tc, hidden_states_words, hidden_states_scales, cos, sin, w_qk_words, w_qk_scales, b_qk, out_0, out_1
):
    nc = tc.nc
    with ExitStack() as ctx:
        ctx.enter_context(tc.manual_schedule())
        keep = ctx.enter_context(tc.tile_pool(name="keep", bufs=1))
        work = ctx.enter_context(tc.tile_pool(name="work", bufs=3))
        outs = ctx.enter_context(tc.tile_pool(name="outs", bufs=8))
        psum = ctx.enter_context(tc.psum_pool(name="psum", bufs=7))
        psum_aux = ctx.enter_context(tc.psum_pool(name="psum_aux", bufs=1))

        chunk_of = {}
        for c, (lo, hi) in enumerate(CHUNKS):
            for i in range(lo, hi):
                chunk_of[i] = c
        tok0 = (CHUNKS[0][1] - CHUNKS[0][0]) * P

        w_code = {}
        w_plane = {}
        h_code = {}
        h_plane = {}
        planes_in_order = []
        for g0, g1 in FIRST_SCALE_RUNS:
            wp = keep.tile([P, g1 - g0, CH], U8, name="wp%d" % g0, tag="wp%d" % g0, align_bytes=1024)
            hp = keep.tile([P, g1 - g0, tok0], U8, name="hp0_%d" % g0, tag="hp0_%d" % g0, align_bytes=1024)
            planes_in_order.append(wp)
            planes_in_order.append(hp)
            for g in range(g0, g1):
                w_plane[g] = (wp, g - g0)
                h_plane[(0, g)] = (hp, g - g0)
        for c in range(1, len(CHUNKS)):
            ntok = (CHUNKS[c][1] - CHUNKS[c][0]) * P
            hp = keep.tile([P, PASSES, ntok], U8, name="hp%d" % c, tag="hp%d" % c, align_bytes=1024)
            planes_in_order.append(hp)
            for g in range(PASSES):
                h_plane[(c, g)] = (hp, g)
        for g0, g1 in FIRST_CODE_RUNS:
            wc = keep.tile([P, g1 - g0, 2 * CH], U8, name="wc%d" % g0, tag="wc%d" % g0, align_bytes=1024)
            hc = keep.tile([P, g1 - g0, 2 * tok0], U8, name="hc0_%d" % g0, tag="hc0_%d" % g0, align_bytes=1024)
            for g in range(g0, g1):
                w_code[g] = (wc, g - g0)
                h_code[(0, g)] = (hc, g - g0)
        lead = keep.tile([P, 1, 2 * LEAD_TILES * P], U8, name="lead", tag="lead", align_bytes=1024)
        for c in range(1, len(CHUNKS)):
            ntok = (CHUNKS[c][1] - CHUNKS[c][0]) * P
            hc = keep.tile([P, PASSES, 2 * ntok], U8, name="hc%d" % c, tag="hc%d" % c, align_bytes=1024)
            for g in range(PASSES):
                h_code[(c, g)] = (hc, g)

        wq_code = keep.tile([P, PASSES, 2 * CH], U8, name="wq_code", tag="wq_code", align_bytes=1024)
        wq_plane = keep.tile([P, PASSES, CH], U8, name="wq_plane", tag="wq_plane", align_bytes=1024)

        ones = keep.tile([P, CH], BF16, name="ones", tag="ones")
        brow = keep.tile([P, CH], BF16, name="brow", tag="brow", align_bytes=64)
        bcol = keep.tile([P, CH], BF16, name="bcol", tag="bcol", align_bytes=64)
        bwide = keep.tile([P, CH], BF16, name="bwide", tag="bwide", align_bytes=64)
        bias = keep.tile([P, CH], BF16, name="bias", tag="bias", align_bytes=64)
        cos_a = keep.tile([P, SWEEP_TILES, HALF], BF16, name="cos_a", tag="cos_a")
        cos_b = keep.tile([P, TILES - SWEEP_TILES, HALF], BF16, name="cos_b", tag="cos_b")
        ss_a = keep.tile([P, SWEEP_TILES, 2, HALF], BF16, name="ss_a", tag="ss_a")
        ss_b = keep.tile([P, TILES - SWEEP_TILES, 2, HALF], BF16, name="ss_b", tag="ss_b")

        nc.vector.memset(ones[:, :], 1.0)
        nc.vector.memset(planes_in_order[0][:, :, :].bitcast(I32), 0)
        nc.vector.memset(planes_in_order[1][:, :, :].bitcast(I32), 0)
        nc.vector.memset(brow[:, :], 0.0)
        for pl in planes_in_order[2:]:
            nc.vector.memset(pl[:, :, :].bitcast(I32), 0)

        cos_v = cos.rearrange("(i p) j -> p i j", p=P)
        sin_v = sin.rearrange("(i p) j -> p i j", p=P)

        def first_codes(k):
            g0, g1 = FIRST_CODE_RUNS[k]
            load_codes(nc, w_code[g0][0], w_qk_words, g0, g1, 0, 2 * CH)
            load_codes(nc, h_code[(0, g0)][0], hidden_states_words, g0, g1, 0, 2 * tok0)

        def first_scales(k):
            g0, g1 = FIRST_SCALE_RUNS[k]
            load_scales(nc, w_plane[g0][0], w_qk_scales, g0, g1, 0, CH)
            load_scales(nc, h_plane[(0, g0)][0], hidden_states_scales, g0, g1, 0, tok0)

        load_codes(nc, w_code[0][0], w_qk_words, 0, 1, 0, 2 * CH)
        load_codes(nc, lead, hidden_states_words, 0, 1, 0, 2 * LEAD_TILES * P)
        first_scales(0)
        nc.sync.dma_start(
            out=h_code[(0, 0)][0][:, :, 2 * LEAD_TILES * P : 2 * tok0].bitcast(I32),
            in_=hidden_states_words[0:1, :, 2 * LEAD_TILES * P : 2 * tok0].rearrange("g p c -> p g c").bitcast(I32),
        )
        first_codes(1)
        first_codes(2)
        nc.sync.dma_start(out=brow[0:P:32, :], in_=b_qk.partition_broadcast(4))
        first_scales(1)
        first_codes(3)
        first_codes(4)
        nc.sync.dma_start(out=cos_a[:, :, :], in_=cos_v[:, 0:SWEEP_TILES, :])
        nc.sync.dma_start(out=ss_a[:, :, 1, :], in_=sin_v[:, 0:SWEEP_TILES, :])
        for c in range(1, len(CHUNKS)):
            t0 = CHUNKS[c][0] * P
            t1 = CHUNKS[c][1] * P
            load_scales(nc, h_plane[(c, 0)][0], hidden_states_scales, 0, PASSES, t0, t1)
            load_codes(nc, h_code[(c, 0)][0], hidden_states_words, 0, PASSES, 2 * t0, 2 * t1)
            if c == 1:
                nc.sync.dma_start(out=cos_b[:, :, :], in_=cos_v[:, SWEEP_TILES:TILES, :])
                nc.sync.dma_start(out=ss_b[:, :, 1, :], in_=sin_v[:, SWEEP_TILES:TILES, :])

        def mm(acc, i, g, n0, n1):
            c = chunk_of[i]
            t = i - CHUNKS[c][0]
            hc, hg = (lead, 0) if (g == 0 and i < LEAD_TILES) else h_code[(c, g)]
            hp, hpg = h_plane[(c, g)]
            wc, wg = w_code[g]
            wp, wpg = w_plane[g]
            nc.tensor.matmul_mx(
                out=acc,
                lhsT=hc[:, hg, 2 * P * t : 2 * P * (t + 1)].bitcast(FP4X4),
                lhsT_scale=hp[:, hpg, P * t : P * (t + 1)],
                rhs=wc[:, wg, 2 * n0 : 2 * n1].bitcast(FP4X4),
                rhs_scale=wp[:, wpg, n0:n1],
                start=(g == 0),
                stop=(g == PASSES - 1),
            )

        def mm_q(acc, i, g, n0, n1):
            c = chunk_of[i]
            t = i - CHUNKS[c][0]
            hc, hg = h_code[(c, g)]
            hp, hpg = h_plane[(c, g)]
            nc.tensor.matmul_mx(
                out=acc,
                lhsT=hc[:, hg, 2 * P * t : 2 * P * (t + 1)].bitcast(FP4X4),
                lhsT_scale=hp[:, hpg, P * t : P * (t + 1)],
                rhs=wq_code[:, g, 2 * n0 : 2 * n1].bitcast(FP4X4),
                rhs_scale=wq_plane[:, g, n0:n1],
                start=(g == 0),
                stop=(g == PASSES - 1),
            )

        def permute_w():
            for runs, table, dst, width in (
                (FIRST_CODE_RUNS, w_code, wq_code, 2 * CH),
                (FIRST_SCALE_RUNS, w_plane, wq_plane, CH),
            ):
                for g0, g1 in runs:
                    for a in range(2):
                        nc.vector.tensor_copy(
                            out=dst[:, g0:g1, a * (width // 2) : (a + 1) * (width // 2)]
                            .bitcast(I32)
                            .rearrange("p g (h c) -> p g h c", h=HEADS),
                            in_=table[g0][0][:, :, :]
                            .bitcast(I32)
                            .rearrange("p g (h a c) -> p g h a c", h=HEADS, a=2)[:, :, :, a, :],
                        )

        def add_bias(i, acc, c0, c1, h0=0, nh=HEADS):
            o = outs.tile([P, nh, c1 - c0], F32, name="o", tag="o")
            nc.vector.tensor_tensor(
                out=o[:, :, :],
                in0=acc.rearrange("p (h d) -> p h d", h=nh),
                in1=bias[:, :].rearrange("p (h d) -> p h d", h=HEADS)[:, h0 : h0 + nh, c0:c1],
                op=ADD,
            )
            return (i, o, c0, c1)

        def store(i, o, c0, c1, queue, h0=0, nh=HEADS):
            rows = slice(i * P, (i + 1) * P)
            if h0 < 2:
                queue.dma_start(out=out_0[rows, :, c0:c1], in_=o[:, 0:2, :])
            if h0 + nh > 2:
                queue.dma_start(out=out_1[rows, :, c0:c1], in_=o[:, 2 - h0 : 4 - h0, :])

        def rotate_products(state):
            i, o, c0, c1 = state
            nh = HEADS
            ct, st, ii = (cos_a, ss_a, i) if i < SWEEP_TILES else (cos_b, ss_b, i - SWEEP_TILES)
            y = o[:, :, 0:ROT].rearrange("p h (a j) -> p h a j", a=2)
            a = work.tile([P, nh, 2, HALF], F32, name="a", tag="a")
            b = work.tile([P, nh, 2, HALF], F32, name="b", tag="b")
            nc.vector.tensor_tensor(
                out=a[:, :, :, :],
                in0=y,
                in1=ct[:, ii, :].unsqueeze(1).unsqueeze(1).to_broadcast([P, nh, 2, HALF]),
                op=MULT,
            )
            nc.vector.tensor_tensor(
                out=b[:, :, :, :],
                in0=y[:, :, ::-1, :],
                in1=st[:, ii, :, :].unsqueeze(1).to_broadcast([P, nh, 2, HALF]),
                op=MULT,
            )
            return (i, o, c0, c1, a, b)

        def finish(state, queue):
            i, o, c0, c1, a, b = state
            nc.vector.tensor_tensor(
                out=o[:, :, 0:ROT],
                in0=a[:, :, :, :].rearrange("p h a j -> p h (a j)"),
                in1=b[:, :, :, :].rearrange("p h a j -> p h (a j)"),
                op=ADD,
            )
            store(i, o, c0, c1, queue)

        pending = []

        def epilogue(i, acc, c0, c1, queue):
            state = add_bias(i, acc, c0, c1)
            if pending:
                finish(pending[0][0], pending[0][1])
                pending.clear()
            if i == 0:
                nc.vector.tensor_scalar_mul(out=ss_a[:, :, 0, :], in0=ss_a[:, :, 1, :], scalar1=-1.0)
            if i == SWEEP_TILES:
                nc.vector.tensor_scalar_mul(out=ss_b[:, :, 0, :], in0=ss_b[:, :, 1, :], scalar1=-1.0)
            pending.append((rotate_products(state), queue))

        aux = psum_aux.tile([P, CH], F32, name="aux", tag="aux")
        for d in range(N_WARM):
            nc.tensor.matmul(out=aux[:, :], lhsT=ones[:, 0:P], rhs=ones[:, :], start=True, stop=True)

        first = []
        for t in range(SWEEP_TILES):
            acc = psum.tile([P, CH], F32, name="acc_f%d" % t, tag="acc")
            first.append(acc)
        for g in range(SWEEP_PASSES):
            for t in range(SWEEP_TILES):
                mm(first[t][:, :], t, g, 0, CH)
            if g == 2:
                nc.vector.transpose(out=bcol[:, :], in_=brow[:, :])
                nc.vector.tensor_copy(
                    out=bwide[:, :].rearrange("p (c i) -> p c i", i=32),
                    in_=bcol[:, :].rearrange("p (c i) -> p c i", i=32)[:, :, 0:1].to_broadcast([P, CH // 32, 32]),
                )
                nc.vector.transpose(out=bias[:, :], in_=bwide[:, :])
        for t in range(SWEEP_TILES):
            for g in range(SWEEP_PASSES, PASSES):
                mm(first[t][:, :], t, g, 0, CH)
            if t == 0:
                permute_w()
            epilogue(t, first[t][:, :], 0, D, nc.sync)
        for i in range(SWEEP_TILES, TILES - SPLIT_TILES):
            acc = psum.tile([P, CH], F32, name="acc", tag="acc")
            for g in range(PASSES):
                mm(acc[:, :], i, g, 0, CH)
            epilogue(i, acc[:, :], 0, D, nc.sync)
        for i in range(TILES - SPLIT_TILES, TILES):
            acc = psum.tile([P, HEADS * ROT], F32, name="acc_r", tag="acc")
            for g in range(PASSES):
                mm_q(acc[:, :], i, g, 0, HEADS * ROT)
            epilogue(i, acc[:, :], 0, ROT, nc.sync)
        for i in range(TILES - SPLIT_TILES, TILES):
            for h0, nh in ([(0, HEADS)] if i < TILES - 1 else [(0, 2), (2, 2)]):
                acc = psum.tile([P, nh * (D - ROT)], F32, name="acc_x", tag="acc")
                n0 = HEADS * ROT + h0 * (D - ROT)
                for g in range(PASSES):
                    mm_q(acc[:, :], i, g, n0, n0 + nh * (D - ROT))
                state = add_bias(i, acc[:, :], ROT, D, h0, nh)
                store(state[0], state[1], state[2], state[3], nc.sync, h0, nh)
                if pending:
                    finish(pending[0][0], pending[0][1])
                    pending.clear()
